import numpy as np
import ml_dtypes


def mxq(x, axis, fmt="e4m3"):
    dtype, down = {"e4m3": (ml_dtypes.float8_e4m3fn, 7), "e5m2": (ml_dtypes.float8_e5m2, 14)}[fmt]
    v = np.moveaxis(np.asarray(x, np.float32).astype(ml_dtypes.bfloat16).astype(np.float64), axis, -1)
    blocks = v.reshape(v.shape[:-1] + (-1, 32))
    amax = np.abs(blocks).max(-1, keepdims=True)
    byte = np.maximum(np.where(amax > 0, np.frexp(amax)[1] - 1 + 127, 0) - down, 1)
    scale = np.exp2(byte - 127.0)
    codes = (blocks / scale).astype(np.float32).astype(dtype).astype(np.float64)
    return np.moveaxis((codes * scale).reshape(v.shape), -1, axis)


WIDE = False


def mx_kscale(k):
    if not WIDE:
        return np.ones(k)
    levels = np.array([10, -10, 5, -5, 0])
    a = np.random.permutation(np.resize(levels, k // 512 * 4)).reshape(k // 512, 4)
    idx = np.arange(k)
    return np.exp2(a[idx // 512, idx % 128 // 32])


BF16 = ml_dtypes.bfloat16


def bf(x):
    return np.asarray(x, np.float32).astype(BF16)


def f64(x):
    return np.asarray(x).astype(np.float64)


E2M1 = np.array([0.0, 0.5, 1.0, 1.5, 2.0, 3.0, 4.0, 6.0, -0.0, -0.5, -1.0, -1.5, -2.0, -3.0, -4.0, -6.0])


def pack_weight(w, fmt):
    k, n = w.shape
    w = f64(bf(w)).reshape(k // 32, 32, n)
    amax = np.abs(w).max(1)
    if fmt == "e4m3":
        byte = np.frexp(amax)[1] - 1 + 127 - 7
    else:
        mant, ex = np.frexp(amax / 6.0)
        byte = np.where(mant > 0.5, ex, ex - 1) + 127
    byte = np.clip(np.where(amax > 0, byte, 1), 1, 254)
    scaled = (w * np.exp2(127.0 - byte)[:, None, :]).reshape(k, n).astype(np.float32)
    by_word = np.ascontiguousarray(scaled.reshape(k // 512, 128, 4, n).transpose(0, 1, 3, 2))
    if fmt == "e4m3":
        words = by_word.astype(ml_dtypes.float8_e4m3fn).view(np.uint8)
    else:
        c = by_word.astype(ml_dtypes.float4_e2m1fn).view(np.uint8) & 0xF
        words = c[..., 0::2] | (c[..., 1::2] << 4)
    return np.ascontiguousarray(words), np.ascontiguousarray(byte.astype(np.uint8).reshape(k // 512, 16, n))


def unpack_weight(words, scales, fmt):
    g, p, n, _ = words.shape
    if fmt == "e4m3":
        vals = np.ascontiguousarray(words).view(ml_dtypes.float8_e4m3fn).astype(np.float64)
    else:
        nib = np.empty((g, p, n, 4), np.uint8)
        nib[..., 0::2] = words & 0xF
        nib[..., 1::2] = words >> 4
        vals = E2M1[nib]
    vals = vals * np.repeat(np.exp2(scales.astype(np.float64) - 127.0), 8, axis=1)[..., None]
    return vals.transpose(0, 1, 3, 2).reshape(g * 512, n)


B, H, L, E, QD = 16, 1, 128, 2048, 128


def setup_inputs():
    s = mx_kscale(E)
    x = bf(np.random.standard_normal((B, H, L, E)) * s)
    Wk_words, Wk_scales = pack_weight((np.random.standard_normal((QD, E)) * 0.3 / np.sqrt(E) / s).T, "e4m3")
    bk = bf(0.1 + 0.1 * np.random.standard_normal(QD))
    Wv_words, Wv_scales = pack_weight((np.random.standard_normal((QD, E)) * 0.3 / np.sqrt(E) / s).T, "e4m3")
    bv = bf(0.1 + 0.1 * np.random.standard_normal(QD))
    return {"x": x,
            "Wk_words": Wk_words,
            "Wk_scales": Wk_scales,
            "bk": bk,
            "Wv_words": Wv_words,
            "Wv_scales": Wv_scales,
            "bv": bv}


def reference(x, Wk_words, Wk_scales, bk, Wv_words, Wv_scales, bv):
    xq = mxq(f64(x), 3, "e4m3")
    K = (xq @ unpack_weight(Wk_words, Wk_scales, "e4m3")) + f64(bk)
    V = (xq @ unpack_weight(Wv_words, Wv_scales, "e4m3")) + f64(bv)
    return K * V

@@ -1,0 +1,139 @@
+from contextlib import ExitStack
+
+import concourse.mybir as mybir
+from concourse.masks import make_identity
+
+F32 = mybir.dt.float32
+BF16 = mybir.dt.bfloat16
+I32 = mybir.dt.int32
+U32 = mybir.dt.uint32
+U8 = mybir.dt.uint8
+FP8X4 = mybir.dt.float8_e4m3fn_x4
+
+P = 128
+PACK = 4
+K_PASS = P * PACK
+ROWS = 16 * 128
+E = 2048
+QD = 128
+PASSES = E // K_PASS
+TILES = ROWS // P
+ROUND = 2
+ROUNDS = TILES // ROUND
+WORDS_PASS = K_PASS // 2
+
+FLOPS = 2 * ROWS * E * 2 * QD
+
+
+def tile_parallelretention_pa_kernel(tc, x, Wk_words, Wk_scales, bk, Wv_words, Wv_scales, bv, out):
+    nc = tc.nc
+    x_rows = x.rearrange("b h l e -> (b h l) e").rearrange("(p t) e -> p t e", t=TILES)
+    out_rows = out.rearrange("b h l n -> (b h l) n").rearrange("(p t) n -> p t n", t=TILES)
+
+    with ExitStack() as ctx:
+        ctx.enter_context(tc.manual_schedule())
+        const = ctx.enter_context(tc.tile_pool(name="const", bufs=1))
+        group_pool = ctx.enter_context(tc.tile_pool(name="group", bufs=4))
+        code_pool = ctx.enter_context(tc.tile_pool(name="code", bufs=6))
+        result_pool = ctx.enter_context(tc.tile_pool(name="result", bufs=3))
+        bank_pool = ctx.enter_context(tc.psum_pool(name="bank", bufs=6))
+        acc_pool = ctx.enter_context(tc.psum_pool(name="acc", bufs=2))
+
+        ident = const.tile([P, P], F32)
+        make_identity(nc, ident[:])
+
+        w_codes = const.tile([P, PASSES, 2, QD], U32, align_bytes=64)
+        w_plane = const.tile([P, PASSES, 2, QD], U8, align_bytes=64)
+        nc.vector.memset(w_plane[:].rearrange("p g w n -> p (g w n)").bitcast(I32), 0)
+        bias = const.tile([P, 2, QD], BF16)
+
+        x_tiles = [const.tile([P, E], BF16, name="x%d" % t) for t in range(TILES)]
+
+        def load_x(t):
+            nc.sync.dma_start(out=x_tiles[t][:], in_=x_rows[:, t, :])
+
+        load_x(0)
+        for quad in range(4):
+            live = slice(32 * quad, 32 * quad + 4)
+            rows = slice(4 * quad, 4 * quad + 4)
+            nc.sync.dma_start(
+                out=w_plane[live, :, 0, :].bitcast(I32),
+                in_=Wk_scales[:, rows, :].rearrange("g r n -> r g n").bitcast(I32),
+            )
+            nc.gpsimd.dma_start(
+                out=w_plane[live, :, 1, :].bitcast(F32),
+                in_=Wv_scales[:, rows, :].rearrange("g r n -> r g n").bitcast(F32),
+            )
+        for t in range(1, 2 * ROUND):
+            load_x(t)
+        nc.sync.dma_start(
+            out=w_codes[:, :, 0, :].bitcast(I32),
+            in_=Wk_words.rearrange("g p n t -> p g (n t)").bitcast(I32),
+        )
+        nc.sync.dma_start(
+            out=w_codes[:, :, 1, :].bitcast(I32),
+            in_=Wv_words.rearrange("g p n t -> p g (n t)").bitcast(I32),
+        )
+        for t in range(2 * ROUND, TILES):
+            load_x(t)
+        nc.gpsimd.dma_start(out=bias[:, 0, :], in_=bk.partition_broadcast(P))
+        nc.gpsimd.dma_start(out=bias[:, 1, :], in_=bv.partition_broadcast(P))
+
+        def quantise_tile(t):
+            words = x_tiles[t][:].bitcast(F32)
+            grouped = group_pool.tile([P, PASSES, P, PACK], BF16, align_bytes=64)
+            for half in range(2):
+                bank = bank_pool.tile([P, 2, 2, P], F32)
+                for gi in range(2):
+                    first = WORDS_PASS * (2 * half + gi)
+                    for u in range(2):
+                        nc.tensor.transpose(
+                            bank[:, gi, u, :], words[:, first + u : first + WORDS_PASS : 2], ident[:]
+                        )
+                nc.scalar.copy(
+                    out=grouped[:].bitcast(F32)[:, 2 * half : 2 * half + 2, :, :],
+                    in_=bank[:].rearrange("p g u r -> p g r u"),
+                )
+            codes = code_pool.tile([P, PASSES, P], U32, align_bytes=64)
+            plane = code_pool.tile([P, PASSES, P], U8, align_bytes=64)
+            nc.vector.quantize_mx(
+                out=codes[:].rearrange("p g r -> p (g r)").bitcast(FP8X4),
+                scales=plane[:].rearrange("p g r -> p (g r)"),
+                in_=grouped[:].rearrange("p g r t -> p (g r t)"),
+            )
+            return codes, plane
+
+        def multiply_round(operands):
+            acc = acc_pool.tile([P, ROUND, 2, QD], F32)
+            for i in range(ROUND):
+                codes, plane = operands[i]
+                for g in range(PASSES):
+                    nc.tensor.matmul_mx(
+                        out=acc[:, i, :, :].rearrange("p w n -> p (w n)"),
+                        lhsT=codes[:, g, :].bitcast(FP8X4),
+                        lhsT_scale=plane[:, g, :],
+                        rhs=w_codes[:, g, :, :].rearrange("p w n -> p (w n)").bitcast(FP8X4),
+                        rhs_scale=w_plane[:, g, :, :].rearrange("p w n -> p (w n)"),
+                        start=(g == 0),
+                        stop=(g == PASSES - 1),
+                    )
+            return acc
+
+        def finish_round(j, acc):
+            sums = result_pool.tile([P, ROUND, 2, QD], F32)
+            nc.vector.tensor_tensor(
+                out=sums[:],
+                in0=acc[:],
+                in1=bias[:].unsqueeze(1).to_broadcast([P, ROUND, 2, QD]),
+                op=mybir.AluOpType.add,
+            )
+            product = result_pool.tile([P, ROUND, QD], F32)
+            nc.vector.tensor_mul(out=product[:], in0=sums[:, :, 0, :], in1=sums[:, :, 1, :])
+            nc.sync.dma_start(out=out_rows[:, ROUND * j : ROUND * (j + 1), :], in_=product[:])
+
+        operands = {}
+        for j in range(ROUNDS + 1):
+            if j < ROUNDS:
+                operands[j] = [quantise_tile(ROUND * j + i) for i in range(ROUND)]
+            if j > 0:
+                finish_round(j - 1, multiply_round(operands[j - 1]))

@@ -52,7 +52,9 @@ def tile_parallelretention_pa_kernel(tc, x, Wk_words, Wk_scales, bk, Wv_words, W
         def load_x(t):
             nc.sync.dma_start(out=x_tiles[t][:], in_=x_rows[:, t, :])
 
-        load_x(0)
+        for half in range(2):
+            cols = slice(half * E // 2, (half + 1) * E // 2)
+            nc.sync.dma_start(out=x_tiles[0][:, cols], in_=x_rows[:, 0, cols])
         for quad in range(4):
             live = slice(32 * quad, 32 * quad + 4)
             rows = slice(4 * quad, 4 * quad + 4)
@@ -74,10 +76,12 @@ def tile_parallelretention_pa_kernel(tc, x, Wk_words, Wk_scales, bk, Wv_words, W
             out=w_codes[:, :, 1, :].bitcast(I32),
             in_=Wv_words.rearrange("g p n t -> p g (n t)").bitcast(I32),
         )
-        for t in range(2 * ROUND, TILES):
+        for t in range(2 * ROUND, 3 * ROUND):
             load_x(t)
-        nc.gpsimd.dma_start(out=bias[:, 0, :], in_=bk.partition_broadcast(P))
-        nc.gpsimd.dma_start(out=bias[:, 1, :], in_=bv.partition_broadcast(P))
+        nc.sync.dma_start(out=bias[:, 0, :], in_=bk.partition_broadcast(P))
+        nc.sync.dma_start(out=bias[:, 1, :], in_=bv.partition_broadcast(P))
+        for t in range(3 * ROUND, TILES):
+            load_x(t)
 
         def quantise_tile(t):
             words = x_tiles[t][:].bitcast(F32)

@@ -43,8 +43,8 @@ def tile_parallelretention_pa_kernel(tc, x, Wk_words, Wk_scales, bk, Wv_words, W
         make_identity(nc, ident[:])
 
         w_codes = const.tile([P, PASSES, 2, QD], U32, align_bytes=64)
-        w_plane = const.tile([P, PASSES, 2, QD], U8, align_bytes=64)
-        nc.vector.memset(w_plane[:].rearrange("p g w n -> p (g w n)").bitcast(I32), 0)
+        w_planes = const.tile([P, 2, QD], U8, align_bytes=64)
+        nc.vector.memset(w_planes[:].rearrange("p w n -> p (w n)").bitcast(I32), 0)
         bias = const.tile([P, 2, QD], BF16)
 
         x_tiles = [const.tile([P, E], BF16, name="x%d" % t) for t in range(TILES)]
@@ -52,22 +52,19 @@ def tile_parallelretention_pa_kernel(tc, x, Wk_words, Wk_scales, bk, Wv_words, W
         def load_x(t):
             nc.sync.dma_start(out=x_tiles[t][:], in_=x_rows[:, t, :])
 
+        def load_scale_quadrant(quad):
+            live = slice(32 * quad, 32 * quad + PACK * PASSES)
+            rows = slice(4 * quad, 4 * quad + 4)
+            nc.sync.dma_start(out=w_planes[live, 0, :].bitcast(I32), in_=Wk_scales[:, rows, :].bitcast(I32))
+            nc.sync.dma_start(out=w_planes[live, 1, :].bitcast(I32), in_=Wv_scales[:, rows, :].bitcast(I32))
+
         for half in range(2):
             cols = slice(half * E // 2, (half + 1) * E // 2)
             nc.sync.dma_start(out=x_tiles[0][:, cols], in_=x_rows[:, 0, cols])
-        for quad in range(4):
-            live = slice(32 * quad, 32 * quad + 4)
-            rows = slice(4 * quad, 4 * quad + 4)
-            nc.sync.dma_start(
-                out=w_plane[live, :, 0, :].bitcast(I32),
-                in_=Wk_scales[:, rows, :].rearrange("g r n -> r g n").bitcast(I32),
-            )
-            nc.gpsimd.dma_start(
-                out=w_plane[live, :, 1, :].bitcast(F32),
-                in_=Wv_scales[:, rows, :].rearrange("g r n -> r g n").bitcast(F32),
-            )
+        load_scale_quadrant(0)
         for t in range(1, 2 * ROUND):
             load_x(t)
+            load_scale_quadrant(t)
         nc.sync.dma_start(
             out=w_codes[:, :, 0, :].bitcast(I32),
             in_=Wk_words.rearrange("g p n t -> p g (n t)").bitcast(I32),
@@ -117,7 +114,7 @@ def tile_parallelretention_pa_kernel(tc, x, Wk_words, Wk_scales, bk, Wv_words, W
                         lhsT=codes[:, g, :].bitcast(FP8X4),
                         lhsT_scale=plane[:, g, :],
                         rhs=w_codes[:, g, :, :].rearrange("p w n -> p (w n)").bitcast(FP8X4),
-                        rhs_scale=w_plane[:, g, :, :].rearrange("p w n -> p (w n)"),
+                        rhs_scale=w_planes[PACK * g : P, :, :].rearrange("p w n -> p (w n)"),
                         start=(g == 0),
                         stop=(g == PASSES - 1),
                     )

@@ -45,7 +45,11 @@ def tile_parallelretention_pa_kernel(tc, x, Wk_words, Wk_scales, bk, Wv_words, W
         w_codes = const.tile([P, PASSES, 2, QD], U32, align_bytes=64)
         w_planes = const.tile([P, 2, QD], U8, align_bytes=64)
         nc.vector.memset(w_planes[:].rearrange("p w n -> p (w n)").bitcast(I32), 0)
-        bias = const.tile([P, 2, QD], BF16)
+        bias_row = const.tile([P, 2, QD], BF16)
+        nc.vector.memset(bias_row[:], 0.0)
+        ones = const.tile([P, P], BF16)
+        nc.vector.memset(ones[:], 1.0)
+        bias = const.tile([P, 2, QD], F32)
 
         x_tiles = [const.tile([P, E], BF16, name="x%d" % t) for t in range(TILES)]
 
@@ -62,6 +66,8 @@ def tile_parallelretention_pa_kernel(tc, x, Wk_words, Wk_scales, bk, Wv_words, W
             cols = slice(half * E // 2, (half + 1) * E // 2)
             nc.sync.dma_start(out=x_tiles[0][:, cols], in_=x_rows[:, 0, cols])
         load_scale_quadrant(0)
+        nc.sync.dma_start(out=bias_row[0:1, 0, :], in_=bk.unsqueeze(0))
+        nc.sync.dma_start(out=bias_row[0:1, 1, :], in_=bv.unsqueeze(0))
         for t in range(1, 2 * ROUND):
             load_x(t)
             load_scale_quadrant(t)
@@ -73,11 +79,7 @@ def tile_parallelretention_pa_kernel(tc, x, Wk_words, Wk_scales, bk, Wv_words, W
             out=w_codes[:, :, 1, :].bitcast(I32),
             in_=Wv_words.rearrange("g p n t -> p g (n t)").bitcast(I32),
         )
-        for t in range(2 * ROUND, 3 * ROUND):
-            load_x(t)
-        nc.sync.dma_start(out=bias[:, 0, :], in_=bk.partition_broadcast(P))
-        nc.sync.dma_start(out=bias[:, 1, :], in_=bv.partition_broadcast(P))
-        for t in range(3 * ROUND, TILES):
+        for t in range(2 * ROUND, TILES):
             load_x(t)
 
         def quantise_tile(t):
@@ -103,6 +105,17 @@ def tile_parallelretention_pa_kernel(tc, x, Wk_words, Wk_scales, bk, Wv_words, W
                 in_=grouped[:].rearrange("p g r t -> p (g r t)"),
             )
             return codes, plane
+
+        def spread_bias():
+            acc = acc_pool.tile([P, ROUND, 2, QD], F32)
+            nc.tensor.matmul(
+                out=acc[:, 0, :, :].rearrange("p w n -> p (w n)"),
+                lhsT=ones[:],
+                rhs=bias_row[:].rearrange("p w n -> p (w n)"),
+                start=True,
+                stop=True,
+            )
+            nc.vector.tensor_copy(out=bias[:], in_=acc[:, 0, :, :])
 
         def multiply_round(operands):
             acc = acc_pool.tile([P, ROUND, 2, QD], F32)
@@ -136,5 +149,7 @@ def tile_parallelretention_pa_kernel(tc, x, Wk_words, Wk_scales, bk, Wv_words, W
         for j in range(ROUNDS + 1):
             if j < ROUNDS:
                 operands[j] = [quantise_tile(ROUND * j + i) for i in range(ROUND)]
+            if j == 1:
+                spread_bias()
             if j > 0:
                 finish_round(j - 1, multiply_round(operands[j - 1]))

@@ -49,7 +49,7 @@ def tile_parallelretention_pa_kernel(tc, x, Wk_words, Wk_scales, bk, Wv_words, W
         nc.vector.memset(bias_row[:], 0.0)
         ones = const.tile([P, P], BF16)
         nc.vector.memset(ones[:], 1.0)
-        bias = const.tile([P, 2, QD], F32)
+        bias = const.tile([P, 2, QD], BF16)
 
         x_tiles = [const.tile([P, E], BF16, name="x%d" % t) for t in range(TILES)]
 
@@ -66,8 +66,6 @@ def tile_parallelretention_pa_kernel(tc, x, Wk_words, Wk_scales, bk, Wv_words, W
             cols = slice(half * E // 2, (half + 1) * E // 2)
             nc.sync.dma_start(out=x_tiles[0][:, cols], in_=x_rows[:, 0, cols])
         load_scale_quadrant(0)
-        nc.sync.dma_start(out=bias_row[0:1, 0, :], in_=bk.unsqueeze(0))
-        nc.sync.dma_start(out=bias_row[0:1, 1, :], in_=bv.unsqueeze(0))
         for t in range(1, 2 * ROUND):
             load_x(t)
             load_scale_quadrant(t)
@@ -79,7 +77,10 @@ def tile_parallelretention_pa_kernel(tc, x, Wk_words, Wk_scales, bk, Wv_words, W
             out=w_codes[:, :, 1, :].bitcast(I32),
             in_=Wv_words.rearrange("g p n t -> p g (n t)").bitcast(I32),
         )
-        for t in range(2 * ROUND, TILES):
+        load_x(2 * ROUND)
+        nc.sync.dma_start(out=bias_row[0:1, 0, :], in_=bk.unsqueeze(0))
+        nc.sync.dma_start(out=bias_row[0:1, 1, :], in_=bv.unsqueeze(0))
+        for t in range(2 * ROUND + 1, TILES):
             load_x(t)
 
         def quantise_tile(t):
@@ -149,7 +150,8 @@ def tile_parallelretention_pa_kernel(tc, x, Wk_words, Wk_scales, bk, Wv_words, W
         for j in range(ROUNDS + 1):
             if j < ROUNDS:
                 operands[j] = [quantise_tile(ROUND * j + i) for i in range(ROUND)]
-            if j == 1:
-                spread_bias()
             if j > 0:
-                finish_round(j - 1, multiply_round(operands[j - 1]))
+                acc = multiply_round(operands[j - 1])
+                if j == 1:
+                    spread_bias()
+                finish_round(j - 1, acc)

@@ -36,8 +36,8 @@ def tile_parallelretention_pa_kernel(tc, x, Wk_words, Wk_scales, bk, Wv_words, W
         group_pool = ctx.enter_context(tc.tile_pool(name="group", bufs=4))
         code_pool = ctx.enter_context(tc.tile_pool(name="code", bufs=6))
         result_pool = ctx.enter_context(tc.tile_pool(name="result", bufs=3))
-        bank_pool = ctx.enter_context(tc.psum_pool(name="bank", bufs=6))
-        acc_pool = ctx.enter_context(tc.psum_pool(name="acc", bufs=2))
+        bank_pool = ctx.enter_context(tc.psum_pool(name="bank", bufs=5))
+        acc_pool = ctx.enter_context(tc.psum_pool(name="acc", bufs=3))
 
         ident = const.tile([P, P], F32)
         make_identity(nc, ident[:])
@@ -77,11 +77,10 @@ def tile_parallelretention_pa_kernel(tc, x, Wk_words, Wk_scales, bk, Wv_words, W
             out=w_codes[:, :, 1, :].bitcast(I32),
             in_=Wv_words.rearrange("g p n t -> p g (n t)").bitcast(I32),
         )
-        load_x(2 * ROUND)
-        nc.sync.dma_start(out=bias_row[0:1, 0, :], in_=bk.unsqueeze(0))
-        nc.sync.dma_start(out=bias_row[0:1, 1, :], in_=bv.unsqueeze(0))
-        for t in range(2 * ROUND + 1, TILES):
+        for t in range(2 * ROUND, TILES):
             load_x(t)
+        nc.gpsimd.dma_start(out=bias_row[0:1, 0, :], in_=bk.unsqueeze(0))
+        nc.gpsimd.dma_start(out=bias_row[0:1, 1, :], in_=bv.unsqueeze(0))
 
         def quantise_tile(t):
             words = x_tiles[t][:].bitcast(F32)
@@ -120,7 +119,7 @@ def tile_parallelretention_pa_kernel(tc, x, Wk_words, Wk_scales, bk, Wv_words, W
 
         def multiply_round(operands):
             acc = acc_pool.tile([P, ROUND, 2, QD], F32)
-            for i in range(ROUND):
+            for i in range(len(operands)):
                 codes, plane = operands[i]
                 for g in range(PASSES):
                     nc.tensor.matmul_mx(
@@ -134,24 +133,27 @@ def tile_parallelretention_pa_kernel(tc, x, Wk_words, Wk_scales, bk, Wv_words, W
                     )
             return acc
 
-        def finish_round(j, acc):
+        def finish_tiles(first, count, acc, multiplier):
             sums = result_pool.tile([P, ROUND, 2, QD], F32)
             nc.vector.tensor_tensor(
-                out=sums[:],
-                in0=acc[:],
-                in1=bias[:].unsqueeze(1).to_broadcast([P, ROUND, 2, QD]),
+                out=sums[:, 0:count, :, :],
+                in0=acc[:, 0:count, :, :],
+                in1=bias[:].unsqueeze(1).to_broadcast([P, count, 2, QD]),
                 op=mybir.AluOpType.add,
             )
             product = result_pool.tile([P, ROUND, QD], F32)
-            nc.vector.tensor_mul(out=product[:], in0=sums[:, :, 0, :], in1=sums[:, :, 1, :])
-            nc.sync.dma_start(out=out_rows[:, ROUND * j : ROUND * (j + 1), :], in_=product[:])
+            multiplier.tensor_mul(out=product[:, 0:count, :], in0=sums[:, 0:count, 0, :], in1=sums[:, 0:count, 1, :])
+            nc.sync.dma_start(out=out_rows[:, first : first + count, :], in_=product[:, 0:count, :])
 
         operands = {}
         for j in range(ROUNDS + 1):
             if j < ROUNDS:
                 operands[j] = [quantise_tile(ROUND * j + i) for i in range(ROUND)]
-            if j > 0:
-                acc = multiply_round(operands[j - 1])
+            if 0 < j < ROUNDS:
                 if j == 1:
                     spread_bias()
-                finish_round(j - 1, acc)
+                acc = multiply_round(operands[j - 1])
+                finish_tiles(ROUND * (j - 1), ROUND, acc, nc.gpsimd if j == ROUNDS - 1 else nc.vector)
+        last = [multiply_round([operand]) for operand in operands[ROUNDS - 1]]
+        for i in range(ROUND):
+            finish_tiles(ROUND * (ROUNDS - 1) + i, 1, last[i], nc.gpsimd if i < ROUND - 1 else nc.vector)

@@ -19,7 +19,8 @@ QD = 128
 PASSES = E // K_PASS
 TILES = ROWS // P
 ROUND = 2
-ROUNDS = TILES // ROUND
+LEAD = 8
+T_RUN = 3
 WORDS_PASS = K_PASS // 2
 
 FLOPS = 2 * ROWS * E * 2 * QD
@@ -82,29 +83,37 @@ def tile_parallelretention_pa_kernel(tc, x, Wk_words, Wk_scales, bk, Wv_words, W
         nc.gpsimd.dma_start(out=bias_row[0:1, 0, :], in_=bk.unsqueeze(0))
         nc.gpsimd.dma_start(out=bias_row[0:1, 1, :], in_=bv.unsqueeze(0))
 
-        def quantise_tile(t):
+        grouped = {}
+        operands = {}
+        sums_bank = {}
+
+        def transpose_half(h):
+            t, half = divmod(h, 2)
             words = x_tiles[t][:].bitcast(F32)
-            grouped = group_pool.tile([P, PASSES, P, PACK], BF16, align_bytes=64)
-            for half in range(2):
-                bank = bank_pool.tile([P, 2, 2, P], F32)
-                for gi in range(2):
-                    first = WORDS_PASS * (2 * half + gi)
-                    for u in range(2):
-                        nc.tensor.transpose(
-                            bank[:, gi, u, :], words[:, first + u : first + WORDS_PASS : 2], ident[:]
-                        )
-                nc.scalar.copy(
-                    out=grouped[:].bitcast(F32)[:, 2 * half : 2 * half + 2, :, :],
-                    in_=bank[:].rearrange("p g u r -> p g r u"),
-                )
+            if half == 0:
+                grouped_tile = group_pool.tile([P, PASSES, P, PACK], BF16, align_bytes=64)
+                grouped[t] = grouped_tile
+            bank = bank_pool.tile([P, 2, 2, P], F32)
+            for gi in range(2):
+                first = WORDS_PASS * (2 * half + gi)
+                for u in range(2):
+                    nc.tensor.transpose(bank[:, gi, u, :], words[:, first + u : first + WORDS_PASS : 2], ident[:])
+            nc.scalar.copy(
+                out=grouped[t][:].bitcast(F32)[:, 2 * half : 2 * half + 2, :, :],
+                in_=bank[:].rearrange("p g u r -> p g r u"),
+            )
+            if half == 1:
+                quantise(t)
+
+        def quantise(t):
             codes = code_pool.tile([P, PASSES, P], U32, align_bytes=64)
             plane = code_pool.tile([P, PASSES, P], U8, align_bytes=64)
             nc.vector.quantize_mx(
                 out=codes[:].rearrange("p g r -> p (g r)").bitcast(FP8X4),
                 scales=plane[:].rearrange("p g r -> p (g r)"),
-                in_=grouped[:].rearrange("p g r t -> p (g r t)"),
+                in_=grouped[t][:].rearrange("p g r t -> p (g r t)"),
             )
-            return codes, plane
+            operands[t] = (codes, plane)
 
         def spread_bias():
             acc = acc_pool.tile([P, ROUND, 2, QD], F32)
@@ -117,21 +126,27 @@ def tile_parallelretention_pa_kernel(tc, x, Wk_words, Wk_scales, bk, Wv_words, W
             )
             nc.vector.tensor_copy(out=bias[:], in_=acc[:, 0, :, :])
 
-        def multiply_round(operands):
-            acc = acc_pool.tile([P, ROUND, 2, QD], F32)
-            for i in range(len(operands)):
-                codes, plane = operands[i]
-                for g in range(PASSES):
-                    nc.tensor.matmul_mx(
-                        out=acc[:, i, :, :].rearrange("p w n -> p (w n)"),
-                        lhsT=codes[:, g, :].bitcast(FP8X4),
-                        lhsT_scale=plane[:, g, :],
-                        rhs=w_codes[:, g, :, :].rearrange("p w n -> p (w n)").bitcast(FP8X4),
-                        rhs_scale=w_planes[PACK * g : P, :, :].rearrange("p w n -> p (w n)"),
-                        start=(g == 0),
-                        stop=(g == PASSES - 1),
-                    )
-            return acc
+        def multiply_pass(m):
+            t, g = divmod(m, PASSES)
+            i = t % ROUND if t < TILES - ROUND else 0
+            if g == 0 and i == 0:
+                acc = acc_pool.tile([P, ROUND, 2, QD], F32)
+                sums_bank[0] = acc
+            codes, plane = operands[t]
+            nc.tensor.matmul_mx(
+                out=sums_bank[0][:, i, :, :].rearrange("p w n -> p (w n)"),
+                lhsT=codes[:, g, :].bitcast(FP8X4),
+                lhsT_scale=plane[:, g, :],
+                rhs=w_codes[:, g, :, :].rearrange("p w n -> p (w n)").bitcast(FP8X4),
+                rhs_scale=w_planes[PACK * g : P, :, :].rearrange("p w n -> p (w n)"),
+                start=(g == 0),
+                stop=(g == PASSES - 1),
+            )
+            if g == PASSES - 1 and t >= TILES - ROUND:
+                finish_tiles(t, 1, sums_bank[0], nc.gpsimd if t < TILES - 1 else nc.vector)
+            elif g == PASSES - 1 and i == ROUND - 1:
+                first = t - ROUND + 1
+                finish_tiles(first, ROUND, sums_bank[0], nc.gpsimd if first == TILES - 2 * ROUND else nc.vector)
 
         def finish_tiles(first, count, acc, multiplier):
             sums = result_pool.tile([P, ROUND, 2, QD], F32)
@@ -145,15 +160,19 @@ def tile_parallelretention_pa_kernel(tc, x, Wk_words, Wk_scales, bk, Wv_words, W
             multiplier.tensor_mul(out=product[:, 0:count, :], in0=sums[:, 0:count, 0, :], in1=sums[:, 0:count, 1, :])
             nc.sync.dma_start(out=out_rows[:, first : first + count, :], in_=product[:, 0:count, :])
 
-        operands = {}
-        for j in range(ROUNDS + 1):
-            if j < ROUNDS:
-                operands[j] = [quantise_tile(ROUND * j + i) for i in range(ROUND)]
-            if 0 < j < ROUNDS:
-                if j == 1:
-                    spread_bias()
-                acc = multiply_round(operands[j - 1])
-                finish_tiles(ROUND * (j - 1), ROUND, acc, nc.gpsimd if j == ROUNDS - 1 else nc.vector)
-        last = [multiply_round([operand]) for operand in operands[ROUNDS - 1]]
-        for i in range(ROUND):
-            finish_tiles(ROUND * (ROUNDS - 1) + i, 1, last[i], nc.gpsimd if i < ROUND - 1 else nc.vector)
+        h = 0
+        m = 0
+        while h < LEAD:
+            transpose_half(h)
+            h += 1
+        spread_bias()
+        while h < 2 * TILES:
+            for i in range(2 * T_RUN):
+                multiply_pass(m)
+                m += 1
+            for i in range(min(T_RUN, 2 * TILES - h)):
+                transpose_half(h)
+                h += 1
+        while m < PASSES * TILES:
+            multiply_pass(m)
+            m += 1

@@ -19,9 +19,10 @@ QD = 128
 PASSES = E // K_PASS
 TILES = ROWS // P
 ROUND = 2
+FIRST_SORTED = 7
+SORT_AHEAD = 3
 LEAD = 8
-T_RUN = 3
-WORDS_PASS = K_PASS // 2
+T_RUN = 4
 
 FLOPS = 2 * ROWS * E * 2 * QD
 
@@ -36,7 +37,8 @@ def tile_parallelretention_pa_kernel(tc, x, Wk_words, Wk_scales, bk, Wv_words, W
         const = ctx.enter_context(tc.tile_pool(name="const", bufs=1))
         group_pool = ctx.enter_context(tc.tile_pool(name="group", bufs=4))
         code_pool = ctx.enter_context(tc.tile_pool(name="code", bufs=6))
-        result_pool = ctx.enter_context(tc.tile_pool(name="result", bufs=3))
+        result_pool = ctx.enter_context(tc.tile_pool(name="result", bufs=8))
+        sort_pool = ctx.enter_context(tc.tile_pool(name="sort", bufs=3))
         bank_pool = ctx.enter_context(tc.psum_pool(name="bank", bufs=5))
         acc_pool = ctx.enter_context(tc.psum_pool(name="acc", bufs=3))
 
@@ -84,26 +86,38 @@ def tile_parallelretention_pa_kernel(tc, x, Wk_words, Wk_scales, bk, Wv_words, W
         nc.gpsimd.dma_start(out=bias_row[0:1, 1, :], in_=bv.unsqueeze(0))
 
         grouped = {}
+        sorted_words = {}
         operands = {}
         sums_bank = {}
 
+        def sort_words(t):
+            ordered = sort_pool.tile([P, PASSES, 2, P], F32)
+            nc.vector.tensor_copy(
+                out=ordered[:].rearrange("p g u w -> p g w u"),
+                in_=x_tiles[t][:].bitcast(F32).rearrange("p (g w u) -> p g w u", g=PASSES, u=2),
+            )
+            sorted_words[t] = ordered
+
         def transpose_half(h):
             t, half = divmod(h, 2)
-            words = x_tiles[t][:].bitcast(F32)
+            words = x_tiles[t][:].bitcast(F32).rearrange("p (g w u) -> p g u w", g=PASSES, u=2)
+            if t in sorted_words:
+                words = sorted_words[t][:]
             if half == 0:
                 grouped_tile = group_pool.tile([P, PASSES, P, PACK], BF16, align_bytes=64)
                 grouped[t] = grouped_tile
             bank = bank_pool.tile([P, 2, 2, P], F32)
             for gi in range(2):
-                first = WORDS_PASS * (2 * half + gi)
                 for u in range(2):
-                    nc.tensor.transpose(bank[:, gi, u, :], words[:, first + u : first + WORDS_PASS : 2], ident[:])
+                    nc.tensor.transpose(bank[:, gi, u, :], words[:, 2 * half + gi, u, :], ident[:])
             nc.scalar.copy(
                 out=grouped[t][:].bitcast(F32)[:, 2 * half : 2 * half + 2, :, :],
                 in_=bank[:].rearrange("p g u r -> p g r u"),
             )
             if half == 1:
                 quantise(t)
+                if t + SORT_AHEAD >= FIRST_SORTED and t % 2 == 0 and t + SORT_AHEAD < TILES:
+                    sort_words(t + SORT_AHEAD)
 
         def quantise(t):
             codes = code_pool.tile([P, PASSES, P], U32, align_bytes=64)

@@ -19,10 +19,9 @@ QD = 128
 PASSES = E // K_PASS
 TILES = ROWS // P
 ROUND = 2
+LEAD = 4
 FIRST_SORTED = 7
 SORT_AHEAD = 3
-LEAD = 8
-T_RUN = 4
 
 FLOPS = 2 * ROWS * E * 2 * QD
 
@@ -88,6 +87,7 @@ def tile_parallelretention_pa_kernel(tc, x, Wk_words, Wk_scales, bk, Wv_words, W
         grouped = {}
         sorted_words = {}
         operands = {}
+        waiting = {}
         sums_bank = {}
 
         def sort_words(t):
@@ -98,8 +98,7 @@ def tile_parallelretention_pa_kernel(tc, x, Wk_words, Wk_scales, bk, Wv_words, W
             )
             sorted_words[t] = ordered
 
-        def transpose_half(h):
-            t, half = divmod(h, 2)
+        def transpose_half(t, half):
             words = x_tiles[t][:].bitcast(F32).rearrange("p (g w u) -> p g u w", g=PASSES, u=2)
             if t in sorted_words:
                 words = sorted_words[t][:]
@@ -114,20 +113,18 @@ def tile_parallelretention_pa_kernel(tc, x, Wk_words, Wk_scales, bk, Wv_words, W
                 out=grouped[t][:].bitcast(F32)[:, 2 * half : 2 * half + 2, :, :],
                 in_=bank[:].rearrange("p g u r -> p g r u"),
             )
-            if half == 1:
-                quantise(t)
-                if t + SORT_AHEAD >= FIRST_SORTED and t % 2 == 0 and t + SORT_AHEAD < TILES:
-                    sort_words(t + SORT_AHEAD)
 
-        def quantise(t):
-            codes = code_pool.tile([P, PASSES, P], U32, align_bytes=64)
-            plane = code_pool.tile([P, PASSES, P], U8, align_bytes=64)
+        def quantise(t, first, count):
+            if first == 0:
+                codes = code_pool.tile([P, PASSES, P], U32, align_bytes=64)
+                plane = code_pool.tile([P, PASSES, P], U8, align_bytes=64)
+                operands[t] = (codes, plane)
+            passes = slice(first, first + count)
             nc.vector.quantize_mx(
-                out=codes[:].rearrange("p g r -> p (g r)").bitcast(FP8X4),
-                scales=plane[:].rearrange("p g r -> p (g r)"),
-                in_=grouped[t][:].rearrange("p g r t -> p (g r t)"),
+                out=operands[t][0][:, passes, :].rearrange("p g r -> p (g r)").bitcast(FP8X4),
+                scales=operands[t][1][:, passes, :].rearrange("p g r -> p (g r)"),
+                in_=grouped[t][:, passes, :, :].rearrange("p g r t -> p (g r t)"),
             )
-            operands[t] = (codes, plane)
 
         def spread_bias():
             acc = acc_pool.tile([P, ROUND, 2, QD], F32)
@@ -140,8 +137,7 @@ def tile_parallelretention_pa_kernel(tc, x, Wk_words, Wk_scales, bk, Wv_words, W
             )
             nc.vector.tensor_copy(out=bias[:], in_=acc[:, 0, :, :])
 
-        def multiply_pass(m):
-            t, g = divmod(m, PASSES)
+        def multiply_pass(t, g):
             i = t % ROUND if t < TILES - ROUND else 0
             if g == 0 and i == 0:
                 acc = acc_pool.tile([P, ROUND, 2, QD], F32)
@@ -157,12 +153,11 @@ def tile_parallelretention_pa_kernel(tc, x, Wk_words, Wk_scales, bk, Wv_words, W
                 stop=(g == PASSES - 1),
             )
             if g == PASSES - 1 and t >= TILES - ROUND:
-                finish_tiles(t, 1, sums_bank[0], nc.gpsimd if t < TILES - 1 else nc.vector)
+                add_biases(t, 1, sums_bank[0])
             elif g == PASSES - 1 and i == ROUND - 1:
-                first = t - ROUND + 1
-                finish_tiles(first, ROUND, sums_bank[0], nc.gpsimd if first == TILES - 2 * ROUND else nc.vector)
+                add_biases(t - ROUND + 1, ROUND, sums_bank[0])
 
-        def finish_tiles(first, count, acc, multiplier):
+        def add_biases(first, count, acc):
             sums = result_pool.tile([P, ROUND, 2, QD], F32)
             nc.vector.tensor_tensor(
                 out=sums[:, 0:count, :, :],
@@ -170,23 +165,44 @@ def tile_parallelretention_pa_kernel(tc, x, Wk_words, Wk_scales, bk, Wv_words, W
                 in1=bias[:].unsqueeze(1).to_broadcast([P, count, 2, QD]),
                 op=mybir.AluOpType.add,
             )
+            if 0 in waiting:
+                multiply_sums(*waiting[0])
+            waiting[0] = (first, count, sums)
+
+        def multiply_sums(first, count, sums):
             product = result_pool.tile([P, ROUND, QD], F32)
-            multiplier.tensor_mul(out=product[:, 0:count, :], in0=sums[:, 0:count, 0, :], in1=sums[:, 0:count, 1, :])
+            nc.vector.tensor_mul(out=product[:, 0:count, :], in0=sums[:, 0:count, 0, :], in1=sums[:, 0:count, 1, :])
             nc.sync.dma_start(out=out_rows[:, first : first + count, :], in_=product[:, 0:count, :])
 
-        h = 0
-        m = 0
-        while h < LEAD:
-            transpose_half(h)
-            h += 1
+        def prepare_tile(t):
+            transpose_half(t, 0)
+            transpose_half(t, 1)
+            quantise(t, 0, PASSES)
+            if t % 2 == 0:
+                if 0 in waiting:
+                    multiply_sums(*waiting[0])
+                    waiting.clear()
+                if FIRST_SORTED <= t + SORT_AHEAD < TILES:
+                    sort_words(t + SORT_AHEAD)
+
+        def multiply_tiles(tiles):
+            for t in tiles:
+                for g in range(PASSES):
+                    multiply_pass(t, g)
+
+        for t in range(LEAD):
+            prepare_tile(t)
         spread_bias()
-        while h < 2 * TILES:
-            for i in range(2 * T_RUN):
-                multiply_pass(m)
-                m += 1
-            for i in range(min(T_RUN, 2 * TILES - h)):
-                transpose_half(h)
-                h += 1
-        while m < PASSES * TILES:
-            multiply_pass(m)
-            m += 1
+        multiplied = 0
+        for run in [[t] for t in range(LEAD, FIRST_SORTED - 1)] + [[t - 1, t] for t in range(FIRST_SORTED, TILES, 2)]:
+            multiply_tiles(range(multiplied, run[0] - 2))
+            multiplied = run[0] - 2
+            for t in run:
+                if t < TILES - 1:
+                    prepare_tile(t)
+        last = TILES - 1
+        for half in range(2):
+            transpose_half(last, half)
+            quantise(last, 2 * half, 2)
+        multiply_tiles(range(multiplied, TILES))
+        multiply_sums(*waiting[0])

@@ -37,7 +37,7 @@ def tile_parallelretention_pa_kernel(tc, x, Wk_words, Wk_scales, bk, Wv_words, W
         group_pool = ctx.enter_context(tc.tile_pool(name="group", bufs=4))
         code_pool = ctx.enter_context(tc.tile_pool(name="code", bufs=6))
         result_pool = ctx.enter_context(tc.tile_pool(name="result", bufs=8))
-        sort_pool = ctx.enter_context(tc.tile_pool(name="sort", bufs=3))
+        sort_pool = ctx.enter_context(tc.tile_pool(name="sort", bufs=6))
         bank_pool = ctx.enter_context(tc.psum_pool(name="bank", bufs=5))
         acc_pool = ctx.enter_context(tc.psum_pool(name="acc", bufs=3))
 
@@ -90,18 +90,19 @@ def tile_parallelretention_pa_kernel(tc, x, Wk_words, Wk_scales, bk, Wv_words, W
         waiting = {}
         sums_bank = {}
 
-        def sort_words(t):
+        def sort_words(t, count, copy):
             ordered = sort_pool.tile([P, PASSES, 2, P], F32)
-            nc.vector.tensor_copy(
-                out=ordered[:].rearrange("p g u w -> p g w u"),
-                in_=x_tiles[t][:].bitcast(F32).rearrange("p (g w u) -> p g w u", g=PASSES, u=2),
+            copy(
+                out=ordered[:, 0:count, :, :].rearrange("p g u w -> p g w u"),
+                in_=x_tiles[t][:].bitcast(F32).rearrange("p (g w u) -> p g w u", g=PASSES, u=2)[:, 0:count, :, :],
             )
-            sorted_words[t] = ordered
+            for g in range(count):
+                sorted_words[t, g] = ordered
 
         def transpose_half(t, half):
             words = x_tiles[t][:].bitcast(F32).rearrange("p (g w u) -> p g u w", g=PASSES, u=2)
-            if t in sorted_words:
-                words = sorted_words[t][:]
+            if (t, 2 * half) in sorted_words:
+                words = sorted_words[t, 2 * half][:]
             if half == 0:
                 grouped_tile = group_pool.tile([P, PASSES, P, PACK], BF16, align_bytes=64)
                 grouped[t] = grouped_tile
@@ -177,13 +178,15 @@ def tile_parallelretention_pa_kernel(tc, x, Wk_words, Wk_scales, bk, Wv_words, W
         def prepare_tile(t):
             transpose_half(t, 0)
             transpose_half(t, 1)
+            if t % 2 == 0 and FIRST_SORTED <= t + 3 < TILES:
+                sort_words(t + 2, 2, nc.scalar.copy)
             quantise(t, 0, PASSES)
             if t % 2 == 0:
                 if 0 in waiting:
                     multiply_sums(*waiting[0])
                     waiting.clear()
                 if FIRST_SORTED <= t + SORT_AHEAD < TILES:
-                    sort_words(t + SORT_AHEAD)
+                    sort_words(t + SORT_AHEAD, PASSES, nc.vector.tensor_copy)
 
         def multiply_tiles(tiles):
             for t in tiles:

@@ -138,6 +138,16 @@ def tile_parallelretention_pa_kernel(tc, x, Wk_words, Wk_scales, bk, Wv_words, W
             )
             nc.vector.tensor_copy(out=bias[:], in_=acc[:, 0, :, :])
 
+        def warm_clock():
+            unread = acc_pool.tile([P, ROUND, 2, QD], F32, name="acc")
+            nc.tensor.matmul(
+                out=unread[:].rearrange("p i w n -> p (i w n)"),
+                lhsT=ones[:],
+                rhs=x_tiles[0][:, 0 : ROUND * 2 * QD],
+                start=True,
+                stop=True,
+            )
+
         def multiply_pass(t, g):
             i = t % ROUND if t < TILES - ROUND else 0
             if g == 0 and i == 0:
@@ -194,6 +204,8 @@ def tile_parallelretention_pa_kernel(tc, x, Wk_words, Wk_scales, bk, Wv_words, W
                     multiply_pass(t, g)
 
         for t in range(LEAD):
+            if t >= LEAD - 2:
+                warm_clock()
             prepare_tile(t)
         spread_bias()
         multiplied = 0

from contextlib import ExitStack

import concourse.mybir as mybir
from concourse.masks import make_identity

F32 = mybir.dt.float32
BF16 = mybir.dt.bfloat16
I32 = mybir.dt.int32
U32 = mybir.dt.uint32
U8 = mybir.dt.uint8
FP8X4 = mybir.dt.float8_e4m3fn_x4

P = 128
PACK = 4
K_PASS = P * PACK
ROWS = 16 * 128
E = 2048
QD = 128
PASSES = E // K_PASS
TILES = ROWS // P
ROUND = 2
LEAD = 4
FIRST_SORTED = 7
SORT_AHEAD = 3

FLOPS = 2 * ROWS * E * 2 * QD


def tile_parallelretention_pa_kernel(tc, x, Wk_words, Wk_scales, bk, Wv_words, Wv_scales, bv, out):
    nc = tc.nc
    x_rows = x.rearrange("b h l e -> (b h l) e").rearrange("(p t) e -> p t e", t=TILES)
    out_rows = out.rearrange("b h l n -> (b h l) n").rearrange("(p t) n -> p t n", t=TILES)

    with ExitStack() as ctx:
        ctx.enter_context(tc.manual_schedule())
        const = ctx.enter_context(tc.tile_pool(name="const", bufs=1))
        group_pool = ctx.enter_context(tc.tile_pool(name="group", bufs=4))
        code_pool = ctx.enter_context(tc.tile_pool(name="code", bufs=6))
        result_pool = ctx.enter_context(tc.tile_pool(name="result", bufs=8))
        sort_pool = ctx.enter_context(tc.tile_pool(name="sort", bufs=6))
        bank_pool = ctx.enter_context(tc.psum_pool(name="bank", bufs=5))
        acc_pool = ctx.enter_context(tc.psum_pool(name="acc", bufs=3))

        ident = const.tile([P, P], F32)
        make_identity(nc, ident[:])

        w_codes = const.tile([P, PASSES, 2, QD], U32, align_bytes=64)
        w_planes = const.tile([P, 2, QD], U8, align_bytes=64)
        nc.vector.memset(w_planes[:].rearrange("p w n -> p (w n)").bitcast(I32), 0)
        bias_row = const.tile([P, 2, QD], BF16)
        nc.vector.memset(bias_row[:], 0.0)
        ones = const.tile([P, P], BF16)
        nc.vector.memset(ones[:], 1.0)
        bias = const.tile([P, 2, QD], BF16)

        x_tiles = [const.tile([P, E], BF16, name="x%d" % t) for t in range(TILES)]

        def load_x(t):
            nc.sync.dma_start(out=x_tiles[t][:], in_=x_rows[:, t, :])

        def load_scale_quadrant(quad):
            live = slice(32 * quad, 32 * quad + PACK * PASSES)
            rows = slice(4 * quad, 4 * quad + 4)
            nc.sync.dma_start(out=w_planes[live, 0, :].bitcast(I32), in_=Wk_scales[:, rows, :].bitcast(I32))
            nc.sync.dma_start(out=w_planes[live, 1, :].bitcast(I32), in_=Wv_scales[:, rows, :].bitcast(I32))

        for half in range(2):
            cols = slice(half * E // 2, (half + 1) * E // 2)
            nc.sync.dma_start(out=x_tiles[0][:, cols], in_=x_rows[:, 0, cols])
        load_scale_quadrant(0)
        for t in range(1, 2 * ROUND):
            load_x(t)
            load_scale_quadrant(t)
        nc.sync.dma_start(
            out=w_codes[:, :, 0, :].bitcast(I32),
            in_=Wk_words.rearrange("g p n t -> p g (n t)").bitcast(I32),
        )
        nc.sync.dma_start(
            out=w_codes[:, :, 1, :].bitcast(I32),
            in_=Wv_words.rearrange("g p n t -> p g (n t)").bitcast(I32),
        )
        for t in range(2 * ROUND, TILES):
            load_x(t)
        nc.gpsimd.dma_start(out=bias_row[0:1, 0, :], in_=bk.unsqueeze(0))
        nc.gpsimd.dma_start(out=bias_row[0:1, 1, :], in_=bv.unsqueeze(0))

        grouped = {}
        sorted_words = {}
        operands = {}
        waiting = {}
        sums_bank = {}

        def sort_words(t, count, copy):
            ordered = sort_pool.tile([P, PASSES, 2, P], F32)
            copy(
                out=ordered[:, 0:count, :, :].rearrange("p g u w -> p g w u"),
                in_=x_tiles[t][:].bitcast(F32).rearrange("p (g w u) -> p g w u", g=PASSES, u=2)[:, 0:count, :, :],
            )
            for g in range(count):
                sorted_words[t, g] = ordered

        def transpose_half(t, half):
            words = x_tiles[t][:].bitcast(F32).rearrange("p (g w u) -> p g u w", g=PASSES, u=2)
            if (t, 2 * half) in sorted_words:
                words = sorted_words[t, 2 * half][:]
            if half == 0:
                grouped_tile = group_pool.tile([P, PASSES, P, PACK], BF16, align_bytes=64)
                grouped[t] = grouped_tile
            bank = bank_pool.tile([P, 2, 2, P], F32)
            for gi in range(2):
                for u in range(2):
                    nc.tensor.transpose(bank[:, gi, u, :], words[:, 2 * half + gi, u, :], ident[:])
            nc.scalar.copy(
                out=grouped[t][:].bitcast(F32)[:, 2 * half : 2 * half + 2, :, :],
                in_=bank[:].rearrange("p g u r -> p g r u"),
            )

        def quantise(t, first, count):
            if first == 0:
                codes = code_pool.tile([P, PASSES, P], U32, align_bytes=64)
                plane = code_pool.tile([P, PASSES, P], U8, align_bytes=64)
                operands[t] = (codes, plane)
            passes = slice(first, first + count)
            nc.vector.quantize_mx(
                out=operands[t][0][:, passes, :].rearrange("p g r -> p (g r)").bitcast(FP8X4),
                scales=operands[t][1][:, passes, :].rearrange("p g r -> p (g r)"),
                in_=grouped[t][:, passes, :, :].rearrange("p g r t -> p (g r t)"),
            )

        def spread_bias():
            acc = acc_pool.tile([P, ROUND, 2, QD], F32)
            nc.tensor.matmul(
                out=acc[:, 0, :, :].rearrange("p w n -> p (w n)"),
                lhsT=ones[:],
                rhs=bias_row[:].rearrange("p w n -> p (w n)"),
                start=True,
                stop=True,
            )
            nc.vector.tensor_copy(out=bias[:], in_=acc[:, 0, :, :])

        def warm_clock():
            unread = acc_pool.tile([P, ROUND, 2, QD], F32, name="acc")
            nc.tensor.matmul(
                out=unread[:].rearrange("p i w n -> p (i w n)"),
                lhsT=ones[:],
                rhs=x_tiles[0][:, 0 : ROUND * 2 * QD],
                start=True,
                stop=True,
            )

        def multiply_pass(t, g):
            i = t % ROUND if t < TILES - ROUND else 0
            if g == 0 and i == 0:
                acc = acc_pool.tile([P, ROUND, 2, QD], F32)
                sums_bank[0] = acc
            codes, plane = operands[t]
            nc.tensor.matmul_mx(
                out=sums_bank[0][:, i, :, :].rearrange("p w n -> p (w n)"),
                lhsT=codes[:, g, :].bitcast(FP8X4),
                lhsT_scale=plane[:, g, :],
                rhs=w_codes[:, g, :, :].rearrange("p w n -> p (w n)").bitcast(FP8X4),
                rhs_scale=w_planes[PACK * g : P, :, :].rearrange("p w n -> p (w n)"),
                start=(g == 0),
                stop=(g == PASSES - 1),
            )
            if g == PASSES - 1 and t >= TILES - ROUND:
                add_biases(t, 1, sums_bank[0])
            elif g == PASSES - 1 and i == ROUND - 1:
                add_biases(t - ROUND + 1, ROUND, sums_bank[0])

        def add_biases(first, count, acc):
            sums = result_pool.tile([P, ROUND, 2, QD], F32)
            nc.vector.tensor_tensor(
                out=sums[:, 0:count, :, :],
                in0=acc[:, 0:count, :, :],
                in1=bias[:].unsqueeze(1).to_broadcast([P, count, 2, QD]),
                op=mybir.AluOpType.add,
            )
            if 0 in waiting:
                multiply_sums(*waiting[0])
            waiting[0] = (first, count, sums)

        def multiply_sums(first, count, sums):
            product = result_pool.tile([P, ROUND, QD], F32)
            nc.vector.tensor_mul(out=product[:, 0:count, :], in0=sums[:, 0:count, 0, :], in1=sums[:, 0:count, 1, :])
            nc.sync.dma_start(out=out_rows[:, first : first + count, :], in_=product[:, 0:count, :])

        def prepare_tile(t):
            transpose_half(t, 0)
            transpose_half(t, 1)
            if t % 2 == 0 and FIRST_SORTED <= t + 3 < TILES:
                sort_words(t + 2, 2, nc.scalar.copy)
            quantise(t, 0, PASSES)
            if t % 2 == 0:
                if 0 in waiting:
                    multiply_sums(*waiting[0])
                    waiting.clear()
                if FIRST_SORTED <= t + SORT_AHEAD < TILES:
                    sort_words(t + SORT_AHEAD, PASSES, nc.vector.tensor_copy)

        def multiply_tiles(tiles):
            for t in tiles:
                for g in range(PASSES):
                    multiply_pass(t, g)

        for t in range(LEAD):
            if t >= LEAD - 2:
                warm_clock()
            prepare_tile(t)
        spread_bias()
        multiplied = 0
        for run in [[t] for t in range(LEAD, FIRST_SORTED - 1)] + [[t - 1, t] for t in range(FIRST_SORTED, TILES, 2)]:
            multiply_tiles(range(multiplied, run[0] - 2))
            multiplied = run[0] - 2
            for t in run:
                if t < TILES - 1:
                    prepare_tile(t)
        last = TILES - 1
        for half in range(2):
            transpose_half(last, half)
            quantise(last, 2 * half, 2)
        multiply_tiles(range(multiplied, TILES))
        multiply_sums(*waiting[0])
